import numpy as np
import ml_dtypes


def mxq(x, axis, fmt="e4m3"):
    dtype, down = {"e4m3": (ml_dtypes.float8_e4m3fn, 7), "e5m2": (ml_dtypes.float8_e5m2, 14)}[fmt]
    v = np.moveaxis(np.asarray(x, np.float32).astype(ml_dtypes.bfloat16).astype(np.float64), axis, -1)
    blocks = v.reshape(v.shape[:-1] + (-1, 32))
    amax = np.abs(blocks).max(-1, keepdims=True)
    byte = np.maximum(np.where(amax > 0, np.frexp(amax)[1] - 1 + 127, 0) - down, 1)
    scale = np.exp2(byte - 127.0)
    codes = (blocks / scale).astype(np.float32).astype(dtype).astype(np.float64)
    return np.moveaxis((codes * scale).reshape(v.shape), -1, axis)


WIDE = False


def mx_kscale(k):
    if not WIDE:
        return np.ones(k)
    levels = np.array([10, -10, 5, -5, 0])
    a = np.random.permutation(np.resize(levels, k // 512 * 4)).reshape(k // 512, 4)
    idx = np.arange(k)
    return np.exp2(a[idx // 512, idx % 128 // 32])


BF16 = ml_dtypes.bfloat16


def bf(x):
    return np.asarray(x, np.float32).astype(BF16)


def f64(x):
    return np.asarray(x).astype(np.float64)


B, P, D = 4096, 2, 512
IN = P * D


def sigmoid(v):
    return 1.0 / (1.0 + np.exp(-v))


def setup_inputs():
    s = mx_kscale(D)
    sf = np.tile(s, P)
    return {"x": bf(np.random.standard_normal((B, IN)) * sf),
            "weights": bf(np.random.standard_normal((P, D, D)) / np.sqrt(D) / s[None, :, None] * s[None, None, :]),
            "bias": bf(np.random.standard_normal(IN) * 0.3 * sf),
            "gain": bf(1.3 + 0.1 * np.random.standard_normal(1)),
            "norm_bias": bf((0.3 + 0.05 * np.random.standard_normal(1)) * s.min()),
            "gamma": bf(0.5 + 0.3 * np.random.standard_normal(IN)),
            "beta": bf(np.random.standard_normal(IN) / sf)}


def reference(x, weights, bias, gain, norm_bias, gamma, beta):
    x, gamma = f64(x), f64(gamma)
    x_norm = x * f64(gain) + f64(norm_bias)
    xp = x_norm.reshape(B, P, D)
    yp = mxq(xp, 2, "e4m3").transpose(1, 0, 2) @ mxq(f64(weights), 1, "e4m3")
    y = yp.transpose(1, 0, 2).reshape(B, IN) + f64(bias)
    mult = gamma + sigmoid(f64(beta) * y) * (1.0 - gamma)
    o = mult * y
    return o + x

@@ -1,0 +1,235 @@
+from contextlib import ExitStack
+
+import concourse.mybir as mybir
+from concourse.masks import make_identity
+
+F32 = mybir.dt.float32
+BF16 = mybir.dt.bfloat16
+U32 = mybir.dt.uint32
+U8 = mybir.dt.uint8
+FP8X4 = mybir.dt.float8_e4m3fn_x4
+ACT = mybir.ActivationFunctionType
+ALU = mybir.AluOpType
+
+P = 128
+B = 4096
+PARTS = 2
+D = 512
+IN = PARTS * D
+ROWS = 512
+JT = ROWS // P
+NBLK = B // ROWS
+NU = NBLK * PARTS
+CC = D // P
+FLOPS = 2 * B * D * D * PARTS
+MANUAL = True
+
+
+def tile_better_transformer_t_kernel(tc, x, weights, bias, gain, norm_bias, gamma, beta, out):
+    nc = tc.nc
+    with ExitStack() as ctx:
+        const = ctx.enter_context(tc.tile_pool(name="const", bufs=1))
+        xin = ctx.enter_context(tc.tile_pool(name="xin", bufs=NBLK))
+        work = ctx.enter_context(tc.tile_pool(name="work", bufs=3))
+        psum = ctx.enter_context(tc.psum_pool(name="psum", bufs=2))
+
+        warm = const.tile([P, 1], F32, name="warm")
+        nc.vector.memset(warm[:], 0.0)
+        nc.scalar.activation(out=warm[:], in_=warm[:], func=ACT.Sigmoid)
+
+        ident = const.tile([P, P], F32, name="ident")
+        make_identity(nc, ident[:])
+
+        prm_bf = const.tile([P, P], BF16, name="prm_bf")
+        nc.vector.memset(prm_bf[:], 0.0)
+        nc.scalar.dma_start(out=prm_bf[0:8, :], in_=bias.rearrange("(r c) -> r c", c=P))
+        nc.scalar.dma_start(out=prm_bf[8:16, :], in_=gamma.rearrange("(r c) -> r c", c=P))
+        nc.scalar.dma_start(out=prm_bf[16:24, :], in_=beta.rearrange("(r c) -> r c", c=P))
+        gain_bf = const.tile([P, 1], BF16, name="gain_bf")
+        nb_bf = const.tile([P, 1], BF16, name="nb_bf")
+        nc.scalar.dma_start(out=gain_bf[:], in_=gain.partition_broadcast(P))
+        nc.scalar.dma_start(out=nb_bf[:], in_=norm_bias.partition_broadcast(P))
+
+        x_sb = []
+        for i in range(NBLK):
+            xt_i = xin.tile([P, JT * IN], BF16, name="x_sb")
+            x_sb.append(xt_i)
+        wraw = const.tile([P, PARTS * 4 * D], BF16, name="wraw")
+
+        def load_x(i):
+            nc.sync.dma_start(
+                out=x_sb[i][:],
+                in_=x[i * ROWS : (i + 1) * ROWS, :].rearrange("(p j) k -> p (j k)", j=JT),
+            )
+
+        for g in range(PARTS):
+            nc.sync.dma_start(
+                out=x_sb[0][:].rearrange("p (j k) -> p j k", j=JT)[:, :, g * D : (g + 1) * D],
+                in_=x[0:ROWS, g * D : (g + 1) * D].rearrange("(p j) k -> p j k", j=JT),
+            )
+            nc.sync.dma_start(
+                out=wraw[:, g * 4 * D : (g + 1) * 4 * D].rearrange("p (u f) -> p u f", u=2),
+                in_=weights[g : g + 1, :, :].rearrange("o (u p e) c -> p (o u) (e c)", u=2, p=P, e=2),
+            )
+        for i in range(1, NBLK):
+            load_x(i)
+
+        gain_f = const.tile([P, 1], F32, name="gain_f")
+        nb_f = const.tile([P, 1], F32, name="nb_f")
+        nc.vector.tensor_copy(out=gain_f[:], in_=gain_bf[:])
+        nc.vector.tensor_copy(out=nb_f[:], in_=nb_bf[:])
+
+        prm_f = const.tile([P, P], F32, name="prm_f")
+        nc.vector.tensor_copy(out=prm_f[:], in_=prm_bf[:])
+        prm_ps = psum.tile([P, 512], F32, name="prm_ps", tag="xt")
+        nc.tensor.transpose(prm_ps[:, 0:P], prm_f[:], ident[:])
+        prm = const.tile([P, 32], F32, name="prm")
+        nc.vector.tensor_copy(out=prm[:], in_=prm_ps[:, 0:32])
+        bb = const.tile([P, 8], F32, name="bb")
+        nc.vector.tensor_tensor(out=bb[:], in0=prm[:, 16:24], in1=prm[:, 0:8], op=ALU.mult)
+        dd = const.tile([P, 8], F32, name="dd")
+        nc.vector.tensor_scalar(out=dd[:], in0=prm[:, 8:16], scalar1=-1.0, scalar2=1.0, op0=ALU.mult, op1=ALU.add)
+
+        wgrp = const.tile([P, PARTS * 4 * D], BF16, name="wgrp", align_bytes=64)
+        wc = const.tile([P, PARTS * D], U32, name="wc", align_bytes=64)
+        ws = const.tile([P, PARTS * D], U8, name="ws", align_bytes=64)
+        for g in range(PARTS):
+            dst = wgrp[:, g * 4 * D : (g + 1) * 4 * D].rearrange("p (c t) -> p c t", t=4)
+            src = wraw[:, g * 4 * D : (g + 1) * 4 * D].rearrange("p (t c) -> p c t", t=4)
+            if g == 0:
+                nc.vector.tensor_copy(out=dst, in_=src)
+            else:
+                nc.scalar.copy(out=dst, in_=src)
+        for g in range(PARTS):
+            nc.vector.quantize_mx(
+                out=wc[:, g * D : (g + 1) * D].bitcast(FP8X4),
+                scales=ws[:, g * D : (g + 1) * D],
+                in_=wgrp[:, g * 4 * D : (g + 1) * 4 * D],
+            )
+
+        xg = {}
+        xc = {}
+        xs = {}
+        acc = {}
+        mm = {}
+        op = {}
+        ob = {}
+        ots = {}
+
+        def stage_a(h, jp):
+            i, g = divmod(h, PARTS)
+            xw = x_sb[i][:].bitcast(F32)
+            if jp == 0:
+                xg[h] = work.tile([P, 4 * ROWS], BF16, name="xg", align_bytes=64)
+            if True:
+                xt = psum.tile([P, 512], F32, name="xt", tag="xt")
+                for u in range(2):
+                    for jj in range(2):
+                        j = 2 * jp + jj
+                        col = j * (IN // 2) + g * (D // 2) + u * P
+                        nc.tensor.transpose(
+                            xt[:, u * 256 + jj * P : u * 256 + (jj + 1) * P], xw[:, col : col + P], ident[:]
+                        )
+                nc.scalar.activation(
+                    out=xg[h][:, jp * 1024 : (jp + 1) * 1024].rearrange("p (n u e) -> p n u e", u=2, e=2),
+                    in_=xt[:].bitcast(BF16).rearrange("p (u n e) -> p n u e", u=2, e=2),
+                    func=ACT.Identity,
+                    scale=gain_f[:, 0:1],
+                    bias=nb_f[:, 0:1],
+                )
+
+        def stage_q(h):
+            xc[h] = work.tile([P, ROWS], U32, name="xc", align_bytes=64)
+            xs[h] = work.tile([P, ROWS], U8, name="xs", align_bytes=64)
+            nc.vector.quantize_mx(out=xc[h][:].bitcast(FP8X4), scales=xs[h][:], in_=xg[h][:])
+
+        def stage_mx(h, k):
+            g = h % PARTS
+            q = g * CC + k
+            a = psum.tile([P, ROWS], F32, name="acc", tag="acc", bufs=4)
+            acc[(h, k)] = a
+            nc.tensor.matmul_mx(
+                out=a[:],
+                lhsT=wc[:, q * P : (q + 1) * P].bitcast(FP8X4),
+                lhsT_scale=ws[:, q * P : (q + 1) * P],
+                rhs=xc[h][:].bitcast(FP8X4),
+                rhs_scale=xs[h][:],
+                start=True,
+                stop=True,
+            )
+            s = work.tile([P, ROWS], F32, name="sg", bufs=4)
+            nc.scalar.activation(
+                out=s[:], in_=a[:], func=ACT.Sigmoid, scale=prm[:, 16 + q : 17 + q], bias=bb[:, q : q + 1]
+            )
+            m = work.tile([P, ROWS], F32, name="mm", bufs=8)
+            mm[(h, k)] = m
+            nc.gpsimd.tensor_scalar(
+                out=m[:], in0=s[:], scalar1=dd[:, q : q + 1], scalar2=prm[:, 8 + q : 9 + q], op0=ALU.mult, op1=ALU.add
+            )
+
+        def stage_prod(h, k):
+            q = (h % PARTS) * CC + k
+            if k == 0:
+                op[h] = work.tile([P, CC * ROWS], F32, name="op")
+            nc.vector.scalar_tensor_tensor(
+                out=op[h][:, k * ROWS : (k + 1) * ROWS],
+                in0=acc[(h, k)][:],
+                scalar=prm[:, q : q + 1],
+                in1=mm[(h, k)][:],
+                op0=ALU.add,
+                op1=ALU.mult,
+            )
+
+        def stage_back(h, j):
+            ot = psum.tile([P, D], F32, name="ot", tag="ot")
+            ots[(h, j)] = ot
+            for k in range(CC):
+                nc.tensor.transpose(
+                    ot[:, k * P : (k + 1) * P], op[h][:, k * ROWS + j * P : k * ROWS + (j + 1) * P], ident[:]
+                )
+
+        def stage_res(h, j):
+            i, g = divmod(h, PARTS)
+            if j == 0:
+                ob[h] = work.tile([P, JT * D], F32, name="ob", bufs=4)
+            nc.vector.tensor_tensor(
+                out=ob[h][:, j * D : (j + 1) * D],
+                in0=ots[(h, j)][:],
+                in1=x_sb[i][:, j * IN + g * D : j * IN + (g + 1) * D],
+                op=ALU.add,
+            )
+            dst = out[i * ROWS : (i + 1) * ROWS, g * D : (g + 1) * D].rearrange("(p j) c -> p j c", j=JT)
+            src = ob[h][:].rearrange("p (j c) -> p j c", j=JT)
+            if h == NU - 1:
+                nc.sync.dma_start(out=dst[:, j : j + 1, :], in_=src[:, j : j + 1, :])
+            elif j == JT - 1:
+                nc.sync.dma_start(out=dst, in_=src)
+
+        def ok(h):
+            return 0 <= h < NU
+
+        def main_loop():
+            for h in range(-3, NU + 1):
+                if ok(h + 2):
+                    stage_q(h + 2)
+                for k in range(CC):
+                    if ok(h):
+                        stage_prod(h, k)
+                    if ok(h + 1):
+                        stage_mx(h + 1, k)
+                    if ok(h - 1):
+                        stage_res(h - 1, k)
+                    if k < 2:
+                        if ok(h - 1):
+                            stage_back(h - 1, k + 2)
+                        if ok(h + 3):
+                            stage_a(h + 3, k)
+                if ok(h):
+                    stage_back(h, 0)
+                    stage_back(h, 1)
+
+        if MANUAL:
+            with tc.manual_schedule():
+                main_loop()
+        else:
+            main_loop()

@@ -22,7 +22,7 @@ NBLK = B // ROWS
 NU = NBLK * PARTS
 CC = D // P
 FLOPS = 2 * B * D * D * PARTS
-MANUAL = True
+MANUAL = False
 
 
 def tile_better_transformer_t_kernel(tc, x, weights, bias, gain, norm_bias, gamma, beta, out):
@@ -33,22 +33,21 @@ def tile_better_transformer_t_kernel(tc, x, weights, bias, gain, norm_bias, gamm
         work = ctx.enter_context(tc.tile_pool(name="work", bufs=3))
         psum = ctx.enter_context(tc.psum_pool(name="psum", bufs=2))
 
-        warm = const.tile([P, 1], F32, name="warm")
-        nc.vector.memset(warm[:], 0.0)
-        nc.scalar.activation(out=warm[:], in_=warm[:], func=ACT.Sigmoid)
-
         ident = const.tile([P, P], F32, name="ident")
         make_identity(nc, ident[:])
 
+        gain_bf = const.tile([P, 1], BF16, name="gain_bf")
+        nb_bf = const.tile([P, 1], BF16, name="nb_bf")
+        nc.scalar.dma_start(out=gain_bf[:], in_=gain.partition_broadcast(P))
+        nc.scalar.dma_start(out=nb_bf[:], in_=norm_bias.partition_broadcast(P))
         prm_bf = const.tile([P, P], BF16, name="prm_bf")
         nc.vector.memset(prm_bf[:], 0.0)
         nc.scalar.dma_start(out=prm_bf[0:8, :], in_=bias.rearrange("(r c) -> r c", c=P))
         nc.scalar.dma_start(out=prm_bf[8:16, :], in_=gamma.rearrange("(r c) -> r c", c=P))
         nc.scalar.dma_start(out=prm_bf[16:24, :], in_=beta.rearrange("(r c) -> r c", c=P))
-        gain_bf = const.tile([P, 1], BF16, name="gain_bf")
-        nb_bf = const.tile([P, 1], BF16, name="nb_bf")
-        nc.scalar.dma_start(out=gain_bf[:], in_=gain.partition_broadcast(P))
-        nc.scalar.dma_start(out=nb_bf[:], in_=norm_bias.partition_broadcast(P))
+        warm = const.tile([P, 1], F32, name="warm")
+        nc.vector.memset(warm[:], 0.0)
+        nc.scalar.activation(out=warm[:], in_=warm[:], func=ACT.Sigmoid)
 
         x_sb = []
         for i in range(NBLK):
@@ -79,34 +78,42 @@ def tile_better_transformer_t_kernel(tc, x, weights, bias, gain, norm_bias, gamm
         nc.vector.tensor_copy(out=gain_f[:], in_=gain_bf[:])
         nc.vector.tensor_copy(out=nb_f[:], in_=nb_bf[:])
 
-        prm_f = const.tile([P, P], F32, name="prm_f")
-        nc.vector.tensor_copy(out=prm_f[:], in_=prm_bf[:])
-        prm_ps = psum.tile([P, 512], F32, name="prm_ps", tag="xt")
-        nc.tensor.transpose(prm_ps[:, 0:P], prm_f[:], ident[:])
-        prm = const.tile([P, 32], F32, name="prm")
-        nc.vector.tensor_copy(out=prm[:], in_=prm_ps[:, 0:32])
-        bb = const.tile([P, 8], F32, name="bb")
-        nc.vector.tensor_tensor(out=bb[:], in0=prm[:, 16:24], in1=prm[:, 0:8], op=ALU.mult)
-        dd = const.tile([P, 8], F32, name="dd")
-        nc.vector.tensor_scalar(out=dd[:], in0=prm[:, 8:16], scalar1=-1.0, scalar2=1.0, op0=ALU.mult, op1=ALU.add)
+        def prep():
+            prm_f = const.tile([P, P], F32, name="prm_f")
+            nc.vector.tensor_copy(out=prm_f[:], in_=prm_bf[:])
+            prm_ps = psum.tile([P, 512], F32, name="prm_ps", tag="xt")
+            nc.tensor.transpose(prm_ps[:, 0:P], prm_f[:], ident[:])
+            prm = const.tile([P, 32], F32, name="prm")
+            nc.vector.tensor_copy(out=prm[:], in_=prm_ps[:, 0:32])
+            bb = const.tile([P, 8], F32, name="bb")
+            nc.vector.tensor_tensor(out=bb[:], in0=prm[:, 16:24], in1=prm[:, 0:8], op=ALU.mult)
+            dd = const.tile([P, 8], F32, name="dd")
+            nc.vector.tensor_scalar(out=dd[:], in0=prm[:, 8:16], scalar1=-1.0, scalar2=1.0, op0=ALU.mult, op1=ALU.add)
 
-        wgrp = const.tile([P, PARTS * 4 * D], BF16, name="wgrp", align_bytes=64)
-        wc = const.tile([P, PARTS * D], U32, name="wc", align_bytes=64)
-        ws = const.tile([P, PARTS * D], U8, name="ws", align_bytes=64)
-        for g in range(PARTS):
-            dst = wgrp[:, g * 4 * D : (g + 1) * 4 * D].rearrange("p (c t) -> p c t", t=4)
-            src = wraw[:, g * 4 * D : (g + 1) * 4 * D].rearrange("p (t c) -> p c t", t=4)
-            if g == 0:
-                nc.vector.tensor_copy(out=dst, in_=src)
-            else:
-                nc.scalar.copy(out=dst, in_=src)
-        for g in range(PARTS):
-            nc.vector.quantize_mx(
-                out=wc[:, g * D : (g + 1) * D].bitcast(FP8X4),
-                scales=ws[:, g * D : (g + 1) * D],
-                in_=wgrp[:, g * 4 * D : (g + 1) * 4 * D],
-            )
+            wgrp = const.tile([P, PARTS * 4 * D], BF16, name="wgrp", align_bytes=64)
+            wc = const.tile([P, PARTS * D], U32, name="wc", align_bytes=64)
+            ws = const.tile([P, PARTS * D], U8, name="ws", align_bytes=64)
+            for g in range(PARTS):
+                dst = wgrp[:, g * 4 * D : (g + 1) * 4 * D].rearrange("p (c t) -> p c t", t=4)
+                src = wraw[:, g * 4 * D : (g + 1) * 4 * D].rearrange("p (t c) -> p c t", t=4)
+                if g == 0:
+                    nc.vector.tensor_copy(out=dst, in_=src)
+                else:
+                    nc.scalar.copy(out=dst, in_=src)
+            for g in range(PARTS):
+                nc.vector.quantize_mx(
+                    out=wc[:, g * D : (g + 1) * D].bitcast(FP8X4),
+                    scales=ws[:, g * D : (g + 1) * D],
+                    in_=wgrp[:, g * 4 * D : (g + 1) * 4 * D],
+                )
 
+            cst["prm"] = prm
+            cst["bb"] = bb
+            cst["dd"] = dd
+            cst["wc"] = wc
+            cst["ws"] = ws
+
+        cst = {}
         xg = {}
         xc = {}
         xs = {}
@@ -130,13 +137,16 @@ def tile_better_transformer_t_kernel(tc, x, weights, bias, gain, norm_bias, gamm
                         nc.tensor.transpose(
                             xt[:, u * 256 + jj * P : u * 256 + (jj + 1) * P], xw[:, col : col + P], ident[:]
                         )
-                nc.scalar.activation(
-                    out=xg[h][:, jp * 1024 : (jp + 1) * 1024].rearrange("p (n u e) -> p n u e", u=2, e=2),
-                    in_=xt[:].bitcast(BF16).rearrange("p (u n e) -> p n u e", u=2, e=2),
-                    func=ACT.Identity,
-                    scale=gain_f[:, 0:1],
-                    bias=nb_f[:, 0:1],
-                )
+                xg_dst = xg[h][:, jp * 1024 : (jp + 1) * 1024].rearrange("p (n u e) -> p n u e", u=2, e=2)
+                xt_src = xt[:].bitcast(BF16).rearrange("p (u n e) -> p n u e", u=2, e=2)
+                if h < 2 and jp == 1:
+                    nc.vector.tensor_scalar(
+                        out=xg_dst, in0=xt_src, scalar1=gain_f[:, 0:1], scalar2=nb_f[:, 0:1], op0=ALU.mult, op1=ALU.add
+                    )
+                else:
+                    nc.scalar.activation(
+                        out=xg_dst, in_=xt_src, func=ACT.Identity, scale=gain_f[:, 0:1], bias=nb_f[:, 0:1]
+                    )
 
         def stage_q(h):
             xc[h] = work.tile([P, ROWS], U32, name="xc", align_bytes=64)
@@ -150,8 +160,8 @@ def tile_better_transformer_t_kernel(tc, x, weights, bias, gain, norm_bias, gamm
             acc[(h, k)] = a
             nc.tensor.matmul_mx(
                 out=a[:],
-                lhsT=wc[:, q * P : (q + 1) * P].bitcast(FP8X4),
-                lhsT_scale=ws[:, q * P : (q + 1) * P],
+                lhsT=cst["wc"][:, q * P : (q + 1) * P].bitcast(FP8X4),
+                lhsT_scale=cst["ws"][:, q * P : (q + 1) * P],
                 rhs=xc[h][:].bitcast(FP8X4),
                 rhs_scale=xs[h][:],
                 start=True,
@@ -159,12 +169,12 @@ def tile_better_transformer_t_kernel(tc, x, weights, bias, gain, norm_bias, gamm
             )
             s = work.tile([P, ROWS], F32, name="sg", bufs=4)
             nc.scalar.activation(
-                out=s[:], in_=a[:], func=ACT.Sigmoid, scale=prm[:, 16 + q : 17 + q], bias=bb[:, q : q + 1]
+                out=s[:], in_=a[:], func=ACT.Sigmoid, scale=cst["prm"][:, 16 + q : 17 + q], bias=cst["bb"][:, q : q + 1]
             )
             m = work.tile([P, ROWS], F32, name="mm", bufs=8)
             mm[(h, k)] = m
             nc.gpsimd.tensor_scalar(
-                out=m[:], in0=s[:], scalar1=dd[:, q : q + 1], scalar2=prm[:, 8 + q : 9 + q], op0=ALU.mult, op1=ALU.add
+                out=m[:], in0=s[:], scalar1=cst["dd"][:, q : q + 1], scalar2=cst["prm"][:, 8 + q : 9 + q], op0=ALU.mult, op1=ALU.add
             )
 
         def stage_prod(h, k):
@@ -174,7 +184,7 @@ def tile_better_transformer_t_kernel(tc, x, weights, bias, gain, norm_bias, gamm
             nc.vector.scalar_tensor_tensor(
                 out=op[h][:, k * ROWS : (k + 1) * ROWS],
                 in0=acc[(h, k)][:],
-                scalar=prm[:, q : q + 1],
+                scalar=cst["prm"][:, q : q + 1],
                 in1=mm[(h, k)][:],
                 op0=ALU.add,
                 op1=ALU.mult,
@@ -192,12 +202,21 @@ def tile_better_transformer_t_kernel(tc, x, weights, bias, gain, norm_bias, gamm
             i, g = divmod(h, PARTS)
             if j == 0:
                 ob[h] = work.tile([P, JT * D], F32, name="ob", bufs=4)
-            nc.vector.tensor_tensor(
-                out=ob[h][:, j * D : (j + 1) * D],
-                in0=ots[(h, j)][:],
-                in1=x_sb[i][:, j * IN + g * D : j * IN + (g + 1) * D],
-                op=ALU.add,
-            )
+            if h % 2 == 1 and j == 1 and h < NU - 1:
+                nc.scalar.copy(out=ob[h][:, j * D : (j + 1) * D], in_=ots[(h, j)][:])
+                nc.gpsimd.tensor_tensor(
+                    out=ob[h][:, j * D : (j + 1) * D],
+                    in0=ob[h][:, j * D : (j + 1) * D],
+                    in1=x_sb[i][:, j * IN + g * D : j * IN + (g + 1) * D],
+                    op=ALU.add,
+                )
+            else:
+                nc.vector.tensor_tensor(
+                    out=ob[h][:, j * D : (j + 1) * D],
+                    in0=ots[(h, j)][:],
+                    in1=x_sb[i][:, j * IN + g * D : j * IN + (g + 1) * D],
+                    op=ALU.add,
+                )
             dst = out[i * ROWS : (i + 1) * ROWS, g * D : (g + 1) * D].rearrange("(p j) c -> p j c", j=JT)
             src = ob[h][:].rearrange("p (j c) -> p j c", j=JT)
             if h == NU - 1:
@@ -227,6 +246,8 @@ def tile_better_transformer_t_kernel(tc, x, weights, bias, gain, norm_bias, gamm
                 if ok(h):
                     stage_back(h, 0)
                     stage_back(h, 1)
+                if h == -3:
+                    prep()
 
         if MANUAL:
             with tc.manual_schedule():

@@ -22,7 +22,8 @@ NBLK = B // ROWS
 NU = NBLK * PARTS
 CC = D // P
 FLOPS = 2 * B * D * D * PARTS
-MANUAL = False
+MANUAL = True
+SHIFT = ((13, 2), (14, 1), (14, 3), (15, 1))
 
 
 def tile_better_transformer_t_kernel(tc, x, weights, bias, gain, norm_bias, gamma, beta, out):
@@ -62,10 +63,13 @@ def tile_better_transformer_t_kernel(tc, x, weights, bias, gain, norm_bias, gamm
             )
 
         for g in range(PARTS):
-            nc.sync.dma_start(
-                out=x_sb[0][:].rearrange("p (j k) -> p j k", j=JT)[:, :, g * D : (g + 1) * D],
-                in_=x[0:ROWS, g * D : (g + 1) * D].rearrange("(p j) k -> p j k", j=JT),
-            )
+            x0_dst = x_sb[0][:].rearrange("p (j k) -> p j k", j=JT)[:, :, g * D : (g + 1) * D]
+            x0_src = x[0:ROWS, g * D : (g + 1) * D].rearrange("(p j) k -> p j k", j=JT)
+            if g == 0:
+                nc.sync.dma_start(out=x0_dst[:, 0:2, :], in_=x0_src[:, 0:2, :])
+                nc.sync.dma_start(out=x0_dst[:, 2:4, :], in_=x0_src[:, 2:4, :])
+            else:
+                nc.sync.dma_start(out=x0_dst, in_=x0_src)
             nc.sync.dma_start(
                 out=wraw[:, g * 4 * D : (g + 1) * 4 * D].rearrange("p (u f) -> p u f", u=2),
                 in_=weights[g : g + 1, :, :].rearrange("o (u p e) c -> p (o u) (e c)", u=2, p=P, e=2),
@@ -78,42 +82,33 @@ def tile_better_transformer_t_kernel(tc, x, weights, bias, gain, norm_bias, gamm
         nc.vector.tensor_copy(out=gain_f[:], in_=gain_bf[:])
         nc.vector.tensor_copy(out=nb_f[:], in_=nb_bf[:])
 
-        def prep():
+        wgrp = const.tile([P, PARTS * 4 * D], BF16, name="wgrp", align_bytes=64)
+        wc = const.tile([P, PARTS * D], U32, name="wc", align_bytes=64)
+        ws = const.tile([P, PARTS * D], U8, name="ws", align_bytes=64)
+        prm = const.tile([P, 32], F32, name="prm")
+        bb = const.tile([P, 8], F32, name="bb")
+        dd = const.tile([P, 8], F32, name="dd")
+
+        def prep_params():
             prm_f = const.tile([P, P], F32, name="prm_f")
             nc.vector.tensor_copy(out=prm_f[:], in_=prm_bf[:])
-            prm_ps = psum.tile([P, 512], F32, name="prm_ps", tag="xt")
+            prm_ps = psum.tile([P, 512], F32, name="prm_ps", tag="ot", bufs=3)
             nc.tensor.transpose(prm_ps[:, 0:P], prm_f[:], ident[:])
-            prm = const.tile([P, 32], F32, name="prm")
             nc.vector.tensor_copy(out=prm[:], in_=prm_ps[:, 0:32])
-            bb = const.tile([P, 8], F32, name="bb")
             nc.vector.tensor_tensor(out=bb[:], in0=prm[:, 16:24], in1=prm[:, 0:8], op=ALU.mult)
-            dd = const.tile([P, 8], F32, name="dd")
             nc.vector.tensor_scalar(out=dd[:], in0=prm[:, 8:16], scalar1=-1.0, scalar2=1.0, op0=ALU.mult, op1=ALU.add)
 
-            wgrp = const.tile([P, PARTS * 4 * D], BF16, name="wgrp", align_bytes=64)
-            wc = const.tile([P, PARTS * D], U32, name="wc", align_bytes=64)
-            ws = const.tile([P, PARTS * D], U8, name="ws", align_bytes=64)
-            for g in range(PARTS):
-                dst = wgrp[:, g * 4 * D : (g + 1) * 4 * D].rearrange("p (c t) -> p c t", t=4)
-                src = wraw[:, g * 4 * D : (g + 1) * 4 * D].rearrange("p (t c) -> p c t", t=4)
-                if g == 0:
-                    nc.vector.tensor_copy(out=dst, in_=src)
-                else:
-                    nc.scalar.copy(out=dst, in_=src)
-            for g in range(PARTS):
-                nc.vector.quantize_mx(
-                    out=wc[:, g * D : (g + 1) * D].bitcast(FP8X4),
-                    scales=ws[:, g * D : (g + 1) * D],
-                    in_=wgrp[:, g * 4 * D : (g + 1) * 4 * D],
-                )
+        def prep_w(g):
+            nc.vector.tensor_copy(
+                out=wgrp[:, g * 4 * D : (g + 1) * 4 * D].rearrange("p (c i t) -> p c t i", i=4, t=4),
+                in_=wraw[:, g * 4 * D : (g + 1) * 4 * D].rearrange("p (t c i) -> p c t i", t=4, i=4),
+            )
+            nc.vector.quantize_mx(
+                out=wc[:, g * D : (g + 1) * D].bitcast(FP8X4),
+                scales=ws[:, g * D : (g + 1) * D],
+                in_=wgrp[:, g * 4 * D : (g + 1) * 4 * D],
+            )
 
-            cst["prm"] = prm
-            cst["bb"] = bb
-            cst["dd"] = dd
-            cst["wc"] = wc
-            cst["ws"] = ws
-
-        cst = {}
         xg = {}
         xc = {}
         xs = {}
@@ -123,13 +118,16 @@ def tile_better_transformer_t_kernel(tc, x, weights, bias, gain, norm_bias, gamm
         ob = {}
         ots = {}
 
-        def stage_a(h, jp):
+        def stage_a(h, jp, early=False):
             i, g = divmod(h, PARTS)
             xw = x_sb[i][:].bitcast(F32)
             if jp == 0:
                 xg[h] = work.tile([P, 4 * ROWS], BF16, name="xg", align_bytes=64)
             if True:
-                xt = psum.tile([P, 512], F32, name="xt", tag="xt")
+                if early:
+                    xt = psum.tile([P, 512], F32, name="xt_e", tag="ot", bufs=3)
+                else:
+                    xt = psum.tile([P, 512], F32, name="xt", tag="xt", bufs=1)
                 for u in range(2):
                     for jj in range(2):
                         j = 2 * jp + jj
@@ -139,7 +137,7 @@ def tile_better_transformer_t_kernel(tc, x, weights, bias, gain, norm_bias, gamm
                         )
                 xg_dst = xg[h][:, jp * 1024 : (jp + 1) * 1024].rearrange("p (n u e) -> p n u e", u=2, e=2)
                 xt_src = xt[:].bitcast(BF16).rearrange("p (u n e) -> p n u e", u=2, e=2)
-                if h < 2 and jp == 1:
+                if False:
                     nc.vector.tensor_scalar(
                         out=xg_dst, in0=xt_src, scalar1=gain_f[:, 0:1], scalar2=nb_f[:, 0:1], op0=ALU.mult, op1=ALU.add
                     )
@@ -160,8 +158,8 @@ def tile_better_transformer_t_kernel(tc, x, weights, bias, gain, norm_bias, gamm
             acc[(h, k)] = a
             nc.tensor.matmul_mx(
                 out=a[:],
-                lhsT=cst["wc"][:, q * P : (q + 1) * P].bitcast(FP8X4),
-                lhsT_scale=cst["ws"][:, q * P : (q + 1) * P],
+                lhsT=wc[:, q * P : (q + 1) * P].bitcast(FP8X4),
+                lhsT_scale=ws[:, q * P : (q + 1) * P],
                 rhs=xc[h][:].bitcast(FP8X4),
                 rhs_scale=xs[h][:],
                 start=True,
@@ -169,12 +167,12 @@ def tile_better_transformer_t_kernel(tc, x, weights, bias, gain, norm_bias, gamm
             )
             s = work.tile([P, ROWS], F32, name="sg", bufs=4)
             nc.scalar.activation(
-                out=s[:], in_=a[:], func=ACT.Sigmoid, scale=cst["prm"][:, 16 + q : 17 + q], bias=cst["bb"][:, q : q + 1]
+                out=s[:], in_=a[:], func=ACT.Sigmoid, scale=prm[:, 16 + q : 17 + q], bias=bb[:, q : q + 1]
             )
             m = work.tile([P, ROWS], F32, name="mm", bufs=8)
             mm[(h, k)] = m
             nc.gpsimd.tensor_scalar(
-                out=m[:], in0=s[:], scalar1=cst["dd"][:, q : q + 1], scalar2=cst["prm"][:, 8 + q : 9 + q], op0=ALU.mult, op1=ALU.add
+                out=m[:], in0=s[:], scalar1=dd[:, q : q + 1], scalar2=prm[:, 8 + q : 9 + q], op0=ALU.mult, op1=ALU.add
             )
 
         def stage_prod(h, k):
@@ -184,14 +182,14 @@ def tile_better_transformer_t_kernel(tc, x, weights, bias, gain, norm_bias, gamm
             nc.vector.scalar_tensor_tensor(
                 out=op[h][:, k * ROWS : (k + 1) * ROWS],
                 in0=acc[(h, k)][:],
-                scalar=cst["prm"][:, q : q + 1],
+                scalar=prm[:, q : q + 1],
                 in1=mm[(h, k)][:],
                 op0=ALU.add,
                 op1=ALU.mult,
             )
 
         def stage_back(h, j):
-            ot = psum.tile([P, D], F32, name="ot", tag="ot")
+            ot = psum.tile([P, D], F32, name="ot", tag="ot", bufs=3)
             ots[(h, j)] = ot
             for k in range(CC):
                 nc.tensor.transpose(
@@ -202,7 +200,7 @@ def tile_better_transformer_t_kernel(tc, x, weights, bias, gain, norm_bias, gamm
             i, g = divmod(h, PARTS)
             if j == 0:
                 ob[h] = work.tile([P, JT * D], F32, name="ob", bufs=4)
-            if h % 2 == 1 and j == 1 and h < NU - 1:
+            if (h, j) in SHIFT:
                 nc.scalar.copy(out=ob[h][:, j * D : (j + 1) * D], in_=ots[(h, j)][:])
                 nc.gpsimd.tensor_tensor(
                     out=ob[h][:, j * D : (j + 1) * D],
@@ -228,26 +226,34 @@ def tile_better_transformer_t_kernel(tc, x, weights, bias, gain, norm_bias, gamm
             return 0 <= h < NU
 
         def main_loop():
-            for h in range(-3, NU + 1):
+            stage_a(0, 0)
+            stage_a(0, 1, True)
+            prep_params()
+            prep_w(0)
+            stage_q(0)
+            stage_a(1, 0, True)
+            stage_a(1, 1, True)
+            for k in range(CC):
+                stage_mx(0, k)
+            prep_w(1)
+            for h in range(0, NU + 1):
                 if ok(h + 2):
-                    stage_q(h + 2)
+                    stage_a(h + 2, 0)
                 for k in range(CC):
                     if ok(h):
                         stage_prod(h, k)
+                    if k == 0 and ok(h + 1):
+                        stage_q(h + 1)
                     if ok(h + 1):
                         stage_mx(h + 1, k)
+                if ok(h + 2):
+                    stage_a(h + 2, 1)
+                for j in range(JT):
                     if ok(h - 1):
-                        stage_res(h - 1, k)
-                    if k < 2:
-                        if ok(h - 1):
-                            stage_back(h - 1, k + 2)
-                        if ok(h + 3):
-                            stage_a(h + 3, k)
-                if ok(h):
-                    stage_back(h, 0)
-                    stage_back(h, 1)
-                if h == -3:
-                    prep()
+                        stage_res(h - 1, j)
+                    hb, jb = divmod(JT * (h - 1) + j + 3, JT)
+                    if ok(hb) and hb <= h:
+                        stage_back(hb, jb)
 
         if MANUAL:
             with tc.manual_schedule():

@@ -23,6 +23,7 @@ NU = NBLK * PARTS
 CC = D // P
 FLOPS = 2 * B * D * D * PARTS
 MANUAL = True
+REPEAT = 2
 SHIFT = ((13, 2), (14, 1), (14, 3), (15, 1))
 
 
@@ -62,18 +63,23 @@ def tile_better_transformer_t_kernel(tc, x, weights, bias, gain, norm_bias, gamm
                 in_=x[i * ROWS : (i + 1) * ROWS, :].rearrange("(p j) k -> p (j k)", j=JT),
             )
 
-        for g in range(PARTS):
-            x0_dst = x_sb[0][:].rearrange("p (j k) -> p j k", j=JT)[:, :, g * D : (g + 1) * D]
-            x0_src = x[0:ROWS, g * D : (g + 1) * D].rearrange("(p j) k -> p j k", j=JT)
-            if g == 0:
-                nc.sync.dma_start(out=x0_dst[:, 0:2, :], in_=x0_src[:, 0:2, :])
-                nc.sync.dma_start(out=x0_dst[:, 2:4, :], in_=x0_src[:, 2:4, :])
-            else:
-                nc.sync.dma_start(out=x0_dst, in_=x0_src)
+        def load_w(g):
             nc.sync.dma_start(
                 out=wraw[:, g * 4 * D : (g + 1) * 4 * D].rearrange("p (u f) -> p u f", u=2),
                 in_=weights[g : g + 1, :, :].rearrange("o (u p e) c -> p (o u) (e c)", u=2, p=P, e=2),
             )
+
+        def load_x0(g, j0, j1):
+            nc.sync.dma_start(
+                out=x_sb[0][:].rearrange("p (j k) -> p j k", j=JT)[:, j0:j1, g * D : (g + 1) * D],
+                in_=x[0:ROWS, g * D : (g + 1) * D].rearrange("(p j) k -> p j k", j=JT)[:, j0:j1, :],
+            )
+
+        load_w(0)
+        load_x0(0, 0, 2)
+        load_x0(0, 2, 4)
+        load_x0(1, 0, 4)
+        load_w(1)
         for i in range(1, NBLK):
             load_x(i)
 
@@ -118,7 +124,7 @@ def tile_better_transformer_t_kernel(tc, x, weights, bias, gain, norm_bias, gamm
         ob = {}
         ots = {}
 
-        def stage_a(h, jp, early=False):
+        def stage_a(h, jp, early=False, on_vector=False):
             i, g = divmod(h, PARTS)
             xw = x_sb[i][:].bitcast(F32)
             if jp == 0:
@@ -137,7 +143,7 @@ def tile_better_transformer_t_kernel(tc, x, weights, bias, gain, norm_bias, gamm
                         )
                 xg_dst = xg[h][:, jp * 1024 : (jp + 1) * 1024].rearrange("p (n u e) -> p n u e", u=2, e=2)
                 xt_src = xt[:].bitcast(BF16).rearrange("p (u n e) -> p n u e", u=2, e=2)
-                if False:
+                if on_vector:
                     nc.vector.tensor_scalar(
                         out=xg_dst, in0=xt_src, scalar1=gain_f[:, 0:1], scalar2=nb_f[:, 0:1], op0=ALU.mult, op1=ALU.add
                     )
@@ -146,25 +152,31 @@ def tile_better_transformer_t_kernel(tc, x, weights, bias, gain, norm_bias, gamm
                         out=xg_dst, in_=xt_src, func=ACT.Identity, scale=gain_f[:, 0:1], bias=nb_f[:, 0:1]
                     )
 
-        def stage_q(h):
-            xc[h] = work.tile([P, ROWS], U32, name="xc", align_bytes=64)
-            xs[h] = work.tile([P, ROWS], U8, name="xs", align_bytes=64)
-            nc.vector.quantize_mx(out=xc[h][:].bitcast(FP8X4), scales=xs[h][:], in_=xg[h][:])
+        def stage_q(h, half):
+            if half == 0:
+                xc[h] = work.tile([P, ROWS], U32, name="xc", align_bytes=64)
+                xs[h] = work.tile([P, ROWS], U8, name="xs", align_bytes=64)
+            n0 = half * (ROWS // 2)
+            n1 = n0 + ROWS // 2
+            nc.vector.quantize_mx(
+                out=xc[h][:, n0:n1].bitcast(FP8X4), scales=xs[h][:, n0:n1], in_=xg[h][:, 4 * n0 : 4 * n1]
+            )
 
         def stage_mx(h, k):
             g = h % PARTS
             q = g * CC + k
             a = psum.tile([P, ROWS], F32, name="acc", tag="acc", bufs=4)
             acc[(h, k)] = a
-            nc.tensor.matmul_mx(
-                out=a[:],
-                lhsT=wc[:, q * P : (q + 1) * P].bitcast(FP8X4),
-                lhsT_scale=ws[:, q * P : (q + 1) * P],
-                rhs=xc[h][:].bitcast(FP8X4),
-                rhs_scale=xs[h][:],
-                start=True,
-                stop=True,
-            )
+            for rep in range(REPEAT):
+                nc.tensor.matmul_mx(
+                    out=a[:],
+                    lhsT=wc[:, q * P : (q + 1) * P].bitcast(FP8X4),
+                    lhsT_scale=ws[:, q * P : (q + 1) * P],
+                    rhs=xc[h][:].bitcast(FP8X4),
+                    rhs_scale=xs[h][:],
+                    start=True,
+                    stop=True,
+                )
             s = work.tile([P, ROWS], F32, name="sg", bufs=4)
             nc.scalar.activation(
                 out=s[:], in_=a[:], func=ACT.Sigmoid, scale=prm[:, 16 + q : 17 + q], bias=bb[:, q : q + 1]
@@ -226,34 +238,39 @@ def tile_better_transformer_t_kernel(tc, x, weights, bias, gain, norm_bias, gamm
             return 0 <= h < NU
 
         def main_loop():
-            stage_a(0, 0)
-            stage_a(0, 1, True)
-            prep_params()
             prep_w(0)
-            stage_q(0)
+            stage_a(0, 0)
+            stage_a(0, 1, True, True)
+            stage_q(0, 0)
+            stage_q(0, 1)
             stage_a(1, 0, True)
-            stage_a(1, 1, True)
+            stage_a(1, 1, True, True)
+            prep_params()
             for k in range(CC):
                 stage_mx(0, k)
             prep_w(1)
+            stage_q(1, 0)
+            stage_q(1, 1)
+            stage_a(2, 0)
             for h in range(0, NU + 1):
-                if ok(h + 2):
-                    stage_a(h + 2, 0)
-                for k in range(CC):
-                    if ok(h):
-                        stage_prod(h, k)
-                    if k == 0 and ok(h + 1):
-                        stage_q(h + 1)
-                    if ok(h + 1):
-                        stage_mx(h + 1, k)
-                if ok(h + 2):
-                    stage_a(h + 2, 1)
-                for j in range(JT):
-                    if ok(h - 1):
-                        stage_res(h - 1, j)
-                    hb, jb = divmod(JT * (h - 1) + j + 3, JT)
-                    if ok(hb) and hb <= h:
-                        stage_back(hb, jb)
+                for half in range(2):
+                    for k in (2 * half, 2 * half + 1):
+                        if ok(h):
+                            stage_prod(h, k)
+                        if ok(h + 1):
+                            stage_mx(h + 1, k)
+                    if h == 0 and half == 0:
+                        stage_a(2, 1, True, True)
+                    if ok(h + 2):
+                        stage_q(h + 2, half)
+                    if ok(h + 3):
+                        stage_a(h + 3, half)
+                    for j in (2 * half, 2 * half + 1):
+                        if ok(h - 1):
+                            stage_res(h - 1, j)
+                        hb, jb = divmod(JT * (h - 1) + j + 2, JT)
+                        if ok(hb):
+                            stage_back(hb, jb)
 
         if MANUAL:
             with tc.manual_schedule():

@@ -24,7 +24,7 @@ CC = D // P
 FLOPS = 2 * B * D * D * PARTS
 MANUAL = True
 REPEAT = 2
-SHIFT = ((13, 2), (14, 1), (14, 3), (15, 1))
+SHIFT = tuple((h, 1) for h in range(NU)) + ((14, 3),)
 
 
 def tile_better_transformer_t_kernel(tc, x, weights, bias, gain, norm_bias, gamma, beta, out):
@@ -152,15 +152,10 @@ def tile_better_transformer_t_kernel(tc, x, weights, bias, gain, norm_bias, gamm
                         out=xg_dst, in_=xt_src, func=ACT.Identity, scale=gain_f[:, 0:1], bias=nb_f[:, 0:1]
                     )
 
-        def stage_q(h, half):
-            if half == 0:
-                xc[h] = work.tile([P, ROWS], U32, name="xc", align_bytes=64)
-                xs[h] = work.tile([P, ROWS], U8, name="xs", align_bytes=64)
-            n0 = half * (ROWS // 2)
-            n1 = n0 + ROWS // 2
-            nc.vector.quantize_mx(
-                out=xc[h][:, n0:n1].bitcast(FP8X4), scales=xs[h][:, n0:n1], in_=xg[h][:, 4 * n0 : 4 * n1]
-            )
+        def stage_q(h):
+            xc[h] = work.tile([P, ROWS], U32, name="xc", align_bytes=64)
+            xs[h] = work.tile([P, ROWS], U8, name="xs", align_bytes=64)
+            nc.vector.quantize_mx(out=xc[h][:].bitcast(FP8X4), scales=xs[h][:], in_=xg[h][:])
 
         def stage_mx(h, k):
             g = h % PARTS
@@ -241,16 +236,14 @@ def tile_better_transformer_t_kernel(tc, x, weights, bias, gain, norm_bias, gamm
             prep_w(0)
             stage_a(0, 0)
             stage_a(0, 1, True, True)
-            stage_q(0, 0)
-            stage_q(0, 1)
+            stage_q(0)
             stage_a(1, 0, True)
             stage_a(1, 1, True, True)
             prep_params()
             for k in range(CC):
                 stage_mx(0, k)
             prep_w(1)
-            stage_q(1, 0)
-            stage_q(1, 1)
+            stage_q(1)
             stage_a(2, 0)
             for h in range(0, NU + 1):
                 for half in range(2):
@@ -261,16 +254,16 @@ def tile_better_transformer_t_kernel(tc, x, weights, bias, gain, norm_bias, gamm
                             stage_mx(h + 1, k)
                     if h == 0 and half == 0:
                         stage_a(2, 1, True, True)
-                    if ok(h + 2):
-                        stage_q(h + 2, half)
-                    if ok(h + 3):
-                        stage_a(h + 3, half)
+                    if half == 0 and ok(h + 2):
+                        stage_q(h + 2)
                     for j in (2 * half, 2 * half + 1):
                         if ok(h - 1):
                             stage_res(h - 1, j)
                         hb, jb = divmod(JT * (h - 1) + j + 2, JT)
                         if ok(hb):
                             stage_back(hb, jb)
+                    if ok(h + 3):
+                        stage_a(h + 3, half)
 
         if MANUAL:
             with tc.manual_schedule():

from contextlib import ExitStack

import concourse.mybir as mybir
from concourse.masks import make_identity

F32 = mybir.dt.float32
BF16 = mybir.dt.bfloat16
U32 = mybir.dt.uint32
U8 = mybir.dt.uint8
FP8X4 = mybir.dt.float8_e4m3fn_x4
ACT = mybir.ActivationFunctionType
ALU = mybir.AluOpType

P = 128
B = 4096
PARTS = 2
D = 512
IN = PARTS * D
ROWS = 512
JT = ROWS // P
NBLK = B // ROWS
NU = NBLK * PARTS
CC = D // P
FLOPS = 2 * B * D * D * PARTS
MANUAL = True
REPEAT = 2
SHIFT = tuple((h, 1) for h in range(NU)) + ((14, 3),)


def tile_better_transformer_t_kernel(tc, x, weights, bias, gain, norm_bias, gamma, beta, out):
    nc = tc.nc
    with ExitStack() as ctx:
        const = ctx.enter_context(tc.tile_pool(name="const", bufs=1))
        xin = ctx.enter_context(tc.tile_pool(name="xin", bufs=NBLK))
        work = ctx.enter_context(tc.tile_pool(name="work", bufs=3))
        psum = ctx.enter_context(tc.psum_pool(name="psum", bufs=2))

        ident = const.tile([P, P], F32, name="ident")
        make_identity(nc, ident[:])

        gain_bf = const.tile([P, 1], BF16, name="gain_bf")
        nb_bf = const.tile([P, 1], BF16, name="nb_bf")
        nc.scalar.dma_start(out=gain_bf[:], in_=gain.partition_broadcast(P))
        nc.scalar.dma_start(out=nb_bf[:], in_=norm_bias.partition_broadcast(P))
        prm_bf = const.tile([P, P], BF16, name="prm_bf")
        nc.vector.memset(prm_bf[:], 0.0)
        nc.scalar.dma_start(out=prm_bf[0:8, :], in_=bias.rearrange("(r c) -> r c", c=P))
        nc.scalar.dma_start(out=prm_bf[8:16, :], in_=gamma.rearrange("(r c) -> r c", c=P))
        nc.scalar.dma_start(out=prm_bf[16:24, :], in_=beta.rearrange("(r c) -> r c", c=P))
        warm = const.tile([P, 1], F32, name="warm")
        nc.vector.memset(warm[:], 0.0)
        nc.scalar.activation(out=warm[:], in_=warm[:], func=ACT.Sigmoid)

        x_sb = []
        for i in range(NBLK):
            xt_i = xin.tile([P, JT * IN], BF16, name="x_sb")
            x_sb.append(xt_i)
        wraw = const.tile([P, PARTS * 4 * D], BF16, name="wraw")

        def load_x(i):
            nc.sync.dma_start(
                out=x_sb[i][:],
                in_=x[i * ROWS : (i + 1) * ROWS, :].rearrange("(p j) k -> p (j k)", j=JT),
            )

        def load_w(g):
            nc.sync.dma_start(
                out=wraw[:, g * 4 * D : (g + 1) * 4 * D].rearrange("p (u f) -> p u f", u=2),
                in_=weights[g : g + 1, :, :].rearrange("o (u p e) c -> p (o u) (e c)", u=2, p=P, e=2),
            )

        def load_x0(g, j0, j1):
            nc.sync.dma_start(
                out=x_sb[0][:].rearrange("p (j k) -> p j k", j=JT)[:, j0:j1, g * D : (g + 1) * D],
                in_=x[0:ROWS, g * D : (g + 1) * D].rearrange("(p j) k -> p j k", j=JT)[:, j0:j1, :],
            )

        load_w(0)
        load_x0(0, 0, 2)
        load_x0(0, 2, 4)
        load_x0(1, 0, 4)
        load_w(1)
        for i in range(1, NBLK):
            load_x(i)

        gain_f = const.tile([P, 1], F32, name="gain_f")
        nb_f = const.tile([P, 1], F32, name="nb_f")
        nc.vector.tensor_copy(out=gain_f[:], in_=gain_bf[:])
        nc.vector.tensor_copy(out=nb_f[:], in_=nb_bf[:])

        wgrp = const.tile([P, PARTS * 4 * D], BF16, name="wgrp", align_bytes=64)
        wc = const.tile([P, PARTS * D], U32, name="wc", align_bytes=64)
        ws = const.tile([P, PARTS * D], U8, name="ws", align_bytes=64)
        prm = const.tile([P, 32], F32, name="prm")
        bb = const.tile([P, 8], F32, name="bb")
        dd = const.tile([P, 8], F32, name="dd")

        def prep_params():
            prm_f = const.tile([P, P], F32, name="prm_f")
            nc.vector.tensor_copy(out=prm_f[:], in_=prm_bf[:])
            prm_ps = psum.tile([P, 512], F32, name="prm_ps", tag="ot", bufs=3)
            nc.tensor.transpose(prm_ps[:, 0:P], prm_f[:], ident[:])
            nc.vector.tensor_copy(out=prm[:], in_=prm_ps[:, 0:32])
            nc.vector.tensor_tensor(out=bb[:], in0=prm[:, 16:24], in1=prm[:, 0:8], op=ALU.mult)
            nc.vector.tensor_scalar(out=dd[:], in0=prm[:, 8:16], scalar1=-1.0, scalar2=1.0, op0=ALU.mult, op1=ALU.add)

        def prep_w(g):
            nc.vector.tensor_copy(
                out=wgrp[:, g * 4 * D : (g + 1) * 4 * D].rearrange("p (c i t) -> p c t i", i=4, t=4),
                in_=wraw[:, g * 4 * D : (g + 1) * 4 * D].rearrange("p (t c i) -> p c t i", t=4, i=4),
            )
            nc.vector.quantize_mx(
                out=wc[:, g * D : (g + 1) * D].bitcast(FP8X4),
                scales=ws[:, g * D : (g + 1) * D],
                in_=wgrp[:, g * 4 * D : (g + 1) * 4 * D],
            )

        xg = {}
        xc = {}
        xs = {}
        acc = {}
        mm = {}
        op = {}
        ob = {}
        ots = {}

        def stage_a(h, jp, early=False, on_vector=False):
            i, g = divmod(h, PARTS)
            xw = x_sb[i][:].bitcast(F32)
            if jp == 0:
                xg[h] = work.tile([P, 4 * ROWS], BF16, name="xg", align_bytes=64)
            if True:
                if early:
                    xt = psum.tile([P, 512], F32, name="xt_e", tag="ot", bufs=3)
                else:
                    xt = psum.tile([P, 512], F32, name="xt", tag="xt", bufs=1)
                for u in range(2):
                    for jj in range(2):
                        j = 2 * jp + jj
                        col = j * (IN // 2) + g * (D // 2) + u * P
                        nc.tensor.transpose(
                            xt[:, u * 256 + jj * P : u * 256 + (jj + 1) * P], xw[:, col : col + P], ident[:]
                        )
                xg_dst = xg[h][:, jp * 1024 : (jp + 1) * 1024].rearrange("p (n u e) -> p n u e", u=2, e=2)
                xt_src = xt[:].bitcast(BF16).rearrange("p (u n e) -> p n u e", u=2, e=2)
                if on_vector:
                    nc.vector.tensor_scalar(
                        out=xg_dst, in0=xt_src, scalar1=gain_f[:, 0:1], scalar2=nb_f[:, 0:1], op0=ALU.mult, op1=ALU.add
                    )
                else:
                    nc.scalar.activation(
                        out=xg_dst, in_=xt_src, func=ACT.Identity, scale=gain_f[:, 0:1], bias=nb_f[:, 0:1]
                    )

        def stage_q(h):
            xc[h] = work.tile([P, ROWS], U32, name="xc", align_bytes=64)
            xs[h] = work.tile([P, ROWS], U8, name="xs", align_bytes=64)
            nc.vector.quantize_mx(out=xc[h][:].bitcast(FP8X4), scales=xs[h][:], in_=xg[h][:])

        def stage_mx(h, k):
            g = h % PARTS
            q = g * CC + k
            a = psum.tile([P, ROWS], F32, name="acc", tag="acc", bufs=4)
            acc[(h, k)] = a
            for rep in range(REPEAT):
                nc.tensor.matmul_mx(
                    out=a[:],
                    lhsT=wc[:, q * P : (q + 1) * P].bitcast(FP8X4),
                    lhsT_scale=ws[:, q * P : (q + 1) * P],
                    rhs=xc[h][:].bitcast(FP8X4),
                    rhs_scale=xs[h][:],
                    start=True,
                    stop=True,
                )
            s = work.tile([P, ROWS], F32, name="sg", bufs=4)
            nc.scalar.activation(
                out=s[:], in_=a[:], func=ACT.Sigmoid, scale=prm[:, 16 + q : 17 + q], bias=bb[:, q : q + 1]
            )
            m = work.tile([P, ROWS], F32, name="mm", bufs=8)
            mm[(h, k)] = m
            nc.gpsimd.tensor_scalar(
                out=m[:], in0=s[:], scalar1=dd[:, q : q + 1], scalar2=prm[:, 8 + q : 9 + q], op0=ALU.mult, op1=ALU.add
            )

        def stage_prod(h, k):
            q = (h % PARTS) * CC + k
            if k == 0:
                op[h] = work.tile([P, CC * ROWS], F32, name="op")
            nc.vector.scalar_tensor_tensor(
                out=op[h][:, k * ROWS : (k + 1) * ROWS],
                in0=acc[(h, k)][:],
                scalar=prm[:, q : q + 1],
                in1=mm[(h, k)][:],
                op0=ALU.add,
                op1=ALU.mult,
            )

        def stage_back(h, j):
            ot = psum.tile([P, D], F32, name="ot", tag="ot", bufs=3)
            ots[(h, j)] = ot
            for k in range(CC):
                nc.tensor.transpose(
                    ot[:, k * P : (k + 1) * P], op[h][:, k * ROWS + j * P : k * ROWS + (j + 1) * P], ident[:]
                )

        def stage_res(h, j):
            i, g = divmod(h, PARTS)
            if j == 0:
                ob[h] = work.tile([P, JT * D], F32, name="ob", bufs=4)
            if (h, j) in SHIFT:
                nc.scalar.copy(out=ob[h][:, j * D : (j + 1) * D], in_=ots[(h, j)][:])
                nc.gpsimd.tensor_tensor(
                    out=ob[h][:, j * D : (j + 1) * D],
                    in0=ob[h][:, j * D : (j + 1) * D],
                    in1=x_sb[i][:, j * IN + g * D : j * IN + (g + 1) * D],
                    op=ALU.add,
                )
            else:
                nc.vector.tensor_tensor(
                    out=ob[h][:, j * D : (j + 1) * D],
                    in0=ots[(h, j)][:],
                    in1=x_sb[i][:, j * IN + g * D : j * IN + (g + 1) * D],
                    op=ALU.add,
                )
            dst = out[i * ROWS : (i + 1) * ROWS, g * D : (g + 1) * D].rearrange("(p j) c -> p j c", j=JT)
            src = ob[h][:].rearrange("p (j c) -> p j c", j=JT)
            if h == NU - 1:
                nc.sync.dma_start(out=dst[:, j : j + 1, :], in_=src[:, j : j + 1, :])
            elif j == JT - 1:
                nc.sync.dma_start(out=dst, in_=src)

        def ok(h):
            return 0 <= h < NU

        def main_loop():
            prep_w(0)
            stage_a(0, 0)
            stage_a(0, 1, True, True)
            stage_q(0)
            stage_a(1, 0, True)
            stage_a(1, 1, True, True)
            prep_params()
            for k in range(CC):
                stage_mx(0, k)
            prep_w(1)
            stage_q(1)
            stage_a(2, 0)
            for h in range(0, NU + 1):
                for half in range(2):
                    for k in (2 * half, 2 * half + 1):
                        if ok(h):
                            stage_prod(h, k)
                        if ok(h + 1):
                            stage_mx(h + 1, k)
                    if h == 0 and half == 0:
                        stage_a(2, 1, True, True)
                    if half == 0 and ok(h + 2):
                        stage_q(h + 2)
                    for j in (2 * half, 2 * half + 1):
                        if ok(h - 1):
                            stage_res(h - 1, j)
                        hb, jb = divmod(JT * (h - 1) + j + 2, JT)
                        if ok(hb):
                            stage_back(hb, jb)
                    if ok(h + 3):
                        stage_a(h + 3, half)

        if MANUAL:
            with tc.manual_schedule():
                main_loop()
        else:
            main_loop()
